import numpy as np
import ml_dtypes


def mxq(x, axis, fmt="e4m3"):
    dtype, down = {"e4m3": (ml_dtypes.float8_e4m3fn, 7), "e5m2": (ml_dtypes.float8_e5m2, 14)}[fmt]
    v = np.moveaxis(np.asarray(x, np.float32).astype(ml_dtypes.bfloat16).astype(np.float64), axis, -1)
    blocks = v.reshape(v.shape[:-1] + (-1, 32))
    amax = np.abs(blocks).max(-1, keepdims=True)
    byte = np.maximum(np.where(amax > 0, np.frexp(amax)[1] - 1 + 127, 0) - down, 1)
    scale = np.exp2(byte - 127.0)
    codes = (blocks / scale).astype(np.float32).astype(dtype).astype(np.float64)
    return np.moveaxis((codes * scale).reshape(v.shape), -1, axis)


WIDE = False


def mx_kscale(k):
    if not WIDE:
        return np.ones(k)
    levels = np.array([10, -10, 5, -5, 0])
    if k % 512:
        return np.exp2(np.random.permutation(np.resize(levels, k // 32))).repeat(32)
    a = np.empty((k // 512, 16))
    for p in range(k // 512):
        a[p, :8] = np.random.permutation(np.resize(levels, 8))
        for g in range(8):
            far = levels[np.abs(levels - a[p, g]) >= 10]
            a[p, g + 8] = far[np.random.randint(len(far))]
    return np.exp2(a.ravel()).repeat(32)


BF16 = ml_dtypes.bfloat16


def bf(x):
    return np.asarray(x, np.float32).astype(BF16)


def f64(x):
    return np.asarray(x).astype(np.float64)


B, D, H, F, C, R = 1024, 4096, 1024, 1024, 128, 32
EPS = 1e-12


def l2norm(x):
    n = np.sqrt((x ** 2).sum(-1, keepdims=True))
    return x / np.maximum(n, EPS)


def draw0():
    s = mx_kscale(H)
    return {"features": bf(np.random.standard_normal((B, H)) * s),
            "ex_features": bf(np.random.standard_normal((D, H)) * s),
            "gW": bf(np.random.standard_normal((F, H)) / np.sqrt(H) / s[None, :]),
            "gb": bf(np.random.standard_normal(F) * 0.1)}


def core(features, ex_features, gW, gb):
    wq = mxq(f64(gW), 1, "e4m3")
    f = (mxq(f64(features), 1, "e4m3") @ wq.T) + f64(gb)
    ex = (mxq(f64(ex_features), 1, "e4m3") @ wq.T) + f64(gb)
    return l2norm(f), l2norm(ex)


def e4m3fn_bytes(y):
    return np.clip(np.asarray(y, np.float64), -448.0, 448.0).astype(np.float32).astype(ml_dtypes.float8_e4m3fn).view(np.uint8)


def e4m3fn_values(b):
    return np.asarray(b, np.uint8).view(ml_dtypes.float8_e4m3fn).astype(np.float64)


def setup_inputs():
    d = draw0()
    x0 = np.asarray(d['ex_features']).astype(np.float64)
    s = (np.max(np.abs(x0), axis=(0,), keepdims=True) / 448.0).astype(np.float32)
    out = {}
    for k, v in d.items():
        if k == 'ex_features':
            out['ex_features_bytes'] = e4m3fn_bytes(x0 / s.astype(np.float64))
            out['ex_features_scale'] = s
        else:
            out[k] = v
    return out


def reference(features, ex_features_bytes, ex_features_scale, gW, gb):
    return core(features, e4m3fn_values(ex_features_bytes) * ex_features_scale.astype(np.float64), gW, gb)

@@ -1,0 +1,299 @@
+from contextlib import ExitStack
+
+import concourse.mybir as mybir
+from concourse.masks import make_identity
+
+F32 = mybir.dt.float32
+BF16 = mybir.dt.bfloat16
+U32 = mybir.dt.uint32
+U8 = mybir.dt.uint8
+FP8 = mybir.dt.float8_e4m3fn
+FP8X4 = mybir.dt.float8_e4m3fn_x4
+ALU = mybir.AluOpType
+ACT = mybir.ActivationFunctionType
+
+P = 128
+K = 1024
+F = 1024
+B_ROWS = 1024
+D_ROWS = 4096
+HALF = 512
+FLOPS = 2 * (B_ROWS + D_ROWS) * K * F
+
+
+def tile_minerva_detex_pa_kernel(tc, features, ex_features_bytes, ex_features_scale, gW, gb, out_0, out_1):
+    nc = tc.nc
+    with ExitStack() as ctx:
+        keep = ctx.enter_context(tc.tile_pool(name="keep", bufs=1))
+        wide = ctx.enter_context(tc.tile_pool(name="wide", bufs=6))
+        grp = ctx.enter_context(tc.tile_pool(name="grp", bufs=3))
+        cod = ctx.enter_context(tc.tile_pool(name="cod", bufs=3))
+        zp = ctx.enter_context(tc.tile_pool(name="zp", bufs=6))
+        jp = ctx.enter_context(tc.tile_pool(name="jp", bufs=2))
+        sp = ctx.enter_context(tc.tile_pool(name="sp", bufs=4))
+        ps_t = ctx.enter_context(tc.psum_pool(name="ps_t", bufs=2))
+        ps_a = ctx.enter_context(tc.psum_pool(name="ps_a", bufs=6))
+        ctx.enter_context(tc.manual_schedule())
+
+        order = []
+        for i in range(4):
+            for c in (2 * i, 2 * i + 1):
+                order.append(("e", c, 0))
+                order.append(("e", c, 1))
+            order.append(("f", i // 2, i % 2))
+        n_pairs = len(order)
+
+        sc4 = keep.tile([P, 2, 4], F32, name="sc4")
+        ex_view = ex_features_bytes.rearrange("(c p n) k -> c p (n k)", p=P, n=4)
+        ex_first = [
+            keep.tile([P, K], U8, name="ex_first0"),
+            keep.tile([P, K], U8, name="ex_first1"),
+            keep.tile([P, 2 * K], U8, name="ex_first2"),
+        ]
+        ex_raw = [None] + [keep.tile([P, 4 * K], U8, name="ex_raw%d" % c) for c in range(1, 8)]
+        f_view = features.rearrange("(c p n) k -> c p n k", p=P, n=4)
+        f_raw = [keep.tile([P, 2, K], BF16, name="f_raw%d" % q) for q in range(4)]
+        w_view = gW.rearrange("(j p) k -> p j k", p=P)
+        w_raw = [keep.tile([P, 2, K], BF16, name="w_raw%d" % i) for i in range(4)]
+        bias_sb = keep.tile([P, F], BF16, name="bias_sb")
+        nc.sync.dma_start(out=ex_first[0][:], in_=ex_view[0][:, 0:K])
+        nc.sync.dma_start(out=sc4[:], in_=ex_features_scale.rearrange("o (g p t) -> p (o g) t", g=2, p=P, t=4))
+        nc.sync.dma_start(out=ex_first[1][:], in_=ex_view[0][:, K:2 * K])
+        nc.sync.dma_start(out=ex_first[2][:], in_=ex_view[0][:, 2 * K:4 * K])
+        for i in range(4):
+            nc.sync.dma_start(out=w_raw[i][:], in_=w_view[:, 2 * i:2 * i + 2, :])
+        nc.sync.dma_start(out=bias_sb[:], in_=gb.partition_broadcast(P))
+        nc.sync.dma_start(out=ex_raw[1][:], in_=ex_view[1])
+        for i in range(4):
+            nc.sync.dma_start(out=f_raw[i][:], in_=f_view[i // 2][:, 2 * (i % 2):2 * (i % 2) + 2, :])
+            if i < 3:
+                nc.sync.dma_start(out=ex_raw[2 * i + 2][:], in_=ex_view[2 * i + 2])
+                nc.sync.dma_start(out=ex_raw[2 * i + 3][:], in_=ex_view[2 * i + 3])
+
+        ident = keep.tile([P, P], F32, name="ident")
+        make_identity(nc, ident[:])
+        one = keep.tile([P, 1], F32, name="one")
+        nc.vector.memset(one[:], 1.0)
+        warm = keep.tile([P, 1], F32, name="warm")
+        nc.scalar.activation(out=warm[:], in_=one[:], func=ACT.Abs_reciprocal_sqrt)
+
+        sc_bc = sc4[:].rearrange("p g (u e) -> p g u e", u=2).unsqueeze(2).to_broadcast([P, 2, P, 2, 2])
+
+        def turn(bank, words):
+            for g in range(2):
+                for u in range(2):
+                    nc.tensor.transpose(
+                        bank[:, (2 * u + g) * P:(2 * u + g + 1) * P],
+                        words[:, 256 * g + u:256 * (g + 1):2],
+                        ident[:],
+                    )
+
+        def empty(bank, dst):
+            nc.scalar.copy(out=dst.bitcast(F32), in_=bank[:].rearrange("p (u g r) -> p g r u", u=2, g=2))
+
+        def empty_scaled(bank, dst):
+            nc.vector.tensor_tensor(
+                out=dst.rearrange("p g r (u e) -> p g r u e", u=2),
+                in0=bank[:].bitcast(BF16).rearrange("p (u g r e) -> p g r u e", u=2, g=2, e=2),
+                in1=sc_bc,
+                op=ALU.mult,
+            )
+
+        w_grp = [keep.tile([P, 2, HALF, 4], BF16, name="w_grp%d" % nh, align_bytes=64) for nh in range(2)]
+        w_cod = [keep.tile([P, 2, HALF], U32, name="w_cod%d" % nh, align_bytes=64) for nh in range(2)]
+        w_scl = [keep.tile([P, 2, HALF], U8, name="w_scl%d" % nh, align_bytes=64) for nh in range(2)]
+        w_bank = {}
+
+        def w_turn(j):
+            bank = ps_a.tile([P, HALF], F32, name="acc")
+            w_bank[j] = bank
+            turn(bank, w_raw[j // 2][:, j % 2, :].bitcast(F32))
+
+        def w_empty(j):
+            empty(w_bank[j], w_grp[j // 4][:, :, (j % 4) * P:(j % 4 + 1) * P, :])
+
+        def w_quant(nh):
+            for g in range(2):
+                nc.vector.quantize_mx(
+                    out=w_cod[nh][:, g, :].bitcast(FP8X4),
+                    scales=w_scl[nh][:, g, :],
+                    in_=w_grp[nh][:, g].rearrange("p n t -> p (n t)"),
+                )
+
+        o0_view = out_0.rearrange("(c p n) f -> c p n f", p=P, n=4)
+        o1_view = out_1.rearrange("(c p n) f -> c p n f", p=P, n=4)
+        xb = {}
+        banks = {}
+        grouped = {}
+        codes = {}
+        accs = {}
+        zs = {}
+        sums = {}
+        floors = {}
+        rinvs = {}
+
+        def st_cast(q, tiles):
+            kind, c, h = order[q]
+            if q not in xb:
+                xb[q] = wide.tile([P, 2, K], BF16, name="xb")
+            t = xb[q]
+            if tiles == 2:
+                nc.scalar.copy(out=t[:].rearrange("p a k -> p (a k)"), in_=ex_raw[c][:, 2 * h * K:(2 * h + 2) * K].bitcast(FP8))
+            elif q == 0:
+                nc.vector.tensor_copy(out=t[:, tiles, :], in_=ex_first[tiles][:].bitcast(FP8))
+            else:
+                nc.scalar.copy(out=t[:, tiles, :], in_=ex_first[2][:, tiles * K:(tiles + 1) * K].bitcast(FP8))
+
+        def st_turn(q, a):
+            kind, c, h = order[q]
+            if kind == "f":
+                words = f_raw[2 * c + h][:, a, :].bitcast(F32)
+            else:
+                words = xb[q][:, a, :].bitcast(F32)
+            bank = ps_t.tile([P, HALF], F32, name="bank")
+            banks[(q, a)] = bank
+            turn(bank, words)
+
+        def st_empty(q, a):
+            if q not in grouped:
+                grouped[q] = grp.tile([P, 2, 2, P, 4], BF16, name="gt", align_bytes=64)
+            if order[q][0] == "f":
+                empty(banks[(q, a)], grouped[q][:, a])
+            else:
+                empty_scaled(banks[(q, a)], grouped[q][:, a])
+
+        def st_quant(q):
+            xc = cod.tile([P, 4 * P], U32, name="xc", align_bytes=64)
+            xs = cod.tile([P, 4 * P], U8, name="xs", align_bytes=64)
+            nc.vector.quantize_mx(out=xc[:].bitcast(FP8X4), scales=xs[:], in_=grouped[q][:].rearrange("p a g r t -> p (a g r t)"))
+            codes[q] = (xc, xs)
+
+        def st_mm(q):
+            xc, xs = codes[q]
+            for a in range(2):
+                for nh in range(2):
+                    acc = ps_a.tile([P, HALF], F32, name="acc")
+                    accs[(q, a, nh)] = acc
+                    for g in range(2):
+                        cols = slice((2 * a + g) * P, (2 * a + g + 1) * P)
+                        nc.tensor.matmul_mx(
+                            out=acc[:],
+                            lhsT=xc[:, cols].bitcast(FP8X4),
+                            lhsT_scale=xs[:, cols],
+                            rhs=w_cod[nh][:, g, :].bitcast(FP8X4),
+                            rhs_scale=w_scl[nh][:, g, :],
+                            start=(g == 0),
+                            stop=(g == 1),
+                        )
+
+        def st_bias(q, a):
+            if q not in zs:
+                zs[q] = zp.tile([P, 2, F], F32, name="z")
+                sums[q] = sp.tile([P, 2], F32, name="ss")
+            z = zs[q]
+            for nh in range(2):
+                nc.vector.tensor_tensor(
+                    out=z[:, a, nh * HALF:(nh + 1) * HALF],
+                    in0=accs[(q, a, nh)][:],
+                    in1=bias_sb[:, nh * HALF:(nh + 1) * HALF],
+                    op=ALU.add,
+                )
+            junk = jp.tile([P, F], BF16, name="junk")
+            nc.scalar.activation(out=junk[:], in_=z[:, a, :], func=ACT.Square, accum_out=sums[q][:, a:a + 1])
+
+        def st_floor(q, eng):
+            sm = sp.tile([P, 2], F32, name="sm")
+            eng.tensor_scalar(out=sm[:], in0=sums[q][:], scalar1=1e-24, scalar2=None, op0=ALU.max)
+            floors[q] = sm
+
+        def st_rnorm(q):
+            ri = sp.tile([P, 2], F32, name="ri")
+            nc.scalar.activation(out=ri[:], in_=floors[q][:], func=ACT.Abs_reciprocal_sqrt)
+            rinvs[q] = ri
+
+        def out_rows(q, a):
+            kind, c, h = order[q]
+            view = o0_view if kind == "f" else o1_view
+            return view[c][:, 2 * h + a, :]
+
+        def st_scale(q):
+            z = zs[q]
+            ri = rinvs[q]
+            for a in range(2):
+                nc.gpsimd.tensor_scalar(out=z[:, a, :], in0=z[:, a, :], scalar1=ri[:, a:a + 1], scalar2=0.0, op0=ALU.mult, op1=ALU.add)
+                nc.sync.dma_start(out=out_rows(q, a), in_=z[:, a, :])
+
+        st_cast(0, 0)
+        st_cast(0, 1)
+        st_turn(0, 0)
+        st_empty(0, 0)
+        st_turn(0, 1)
+        st_empty(0, 1)
+        st_cast(1, 0)
+        st_cast(1, 1)
+        w_turn(0)
+        w_turn(1)
+        st_quant(0)
+        st_turn(1, 0)
+        st_empty(1, 0)
+        w_turn(2)
+        w_turn(3)
+        st_turn(1, 1)
+        st_empty(1, 1)
+        w_turn(4)
+        w_turn(5)
+        w_empty(0)
+        w_turn(6)
+        w_empty(1)
+        w_turn(7)
+        w_empty(2)
+        w_empty(3)
+        st_quant(1)
+        w_quant(0)
+        for j in range(4, 8):
+            w_empty(j)
+        w_quant(1)
+        st_cast(2, 2)
+        st_mm(0)
+
+        for s in range(n_pairs):
+            last = s == n_pairs - 1
+            plain_next = s + 2 < n_pairs and order[s + 2][0] == "f"
+            if s + 2 < n_pairs:
+                st_turn(s + 2, 0)
+                st_turn(s + 2, 1)
+            if plain_next:
+                st_empty(s + 2, 0)
+                st_rnorm(s - 1)
+                st_scale(s - 1)
+                st_empty(s + 2, 1)
+            st_bias(s, 0)
+            if s + 1 < n_pairs:
+                if s > 0:
+                    st_quant(s + 1)
+                st_mm(s + 1)
+            if s > 0 and not plain_next:
+                st_rnorm(s - 1)
+                st_scale(s - 1)
+            st_bias(s, 1)
+            if not last:
+                st_floor(s, nc.gpsimd)
+            if s + 2 < n_pairs and not plain_next:
+                st_empty(s + 2, 0)
+                st_empty(s + 2, 1)
+            if s == 0:
+                st_cast(3, 2)
+            if s + 4 < n_pairs and order[s + 4][0] == "e":
+                st_cast(s + 4, 2)
+
+        q = n_pairs - 1
+        st_floor(q, nc.vector)
+        st_rnorm(q)
+        z = zs[q]
+        ri = rinvs[q]
+        nc.vector.tensor_scalar(out=z[:, 0, :], in0=z[:, 0, :], scalar1=ri[:, 0:1], scalar2=None, op0=ALU.mult)
+        nc.sync.dma_start(out=out_rows(q, 0), in_=z[:, 0, :])
+        nc.scalar.activation(out=z[:, 1, HALF:F], in_=z[:, 1, HALF:F], func=ACT.Copy, scale=ri[:, 1:2])
+        nc.sync.dma_start(out=out_rows(q, 1)[:, HALF:F], in_=z[:, 1, HALF:F])
+        nc.vector.tensor_scalar(out=z[:, 1, 0:HALF], in0=z[:, 1, 0:HALF], scalar1=ri[:, 1:2], scalar2=None, op0=ALU.mult)
+        nc.sync.dma_start(out=out_rows(q, 1)[:, 0:HALF], in_=z[:, 1, 0:HALF])

@@ -25,7 +25,7 @@ def tile_minerva_detex_pa_kernel(tc, features, ex_features_bytes, ex_features_sc
     nc = tc.nc
     with ExitStack() as ctx:
         keep = ctx.enter_context(tc.tile_pool(name="keep", bufs=1))
-        wide = ctx.enter_context(tc.tile_pool(name="wide", bufs=6))
+        wide = ctx.enter_context(tc.tile_pool(name="wide", bufs=8))
         grp = ctx.enter_context(tc.tile_pool(name="grp", bufs=3))
         cod = ctx.enter_context(tc.tile_pool(name="cod", bufs=3))
         zp = ctx.enter_context(tc.tile_pool(name="zp", bufs=6))
@@ -283,8 +283,10 @@ def tile_minerva_detex_pa_kernel(tc, features, ex_features_bytes, ex_features_sc
                 st_empty(s + 2, 1)
             if s == 0:
                 st_cast(3, 2)
-            if s + 4 < n_pairs and order[s + 4][0] == "e":
+            if s + 4 < n_pairs and order[s + 4][0] == "e" and not plain_next:
                 st_cast(s + 4, 2)
+            if s + 6 < n_pairs and order[s + 4][0] == "f":
+                st_cast(s + 6, 2)
 
         q = n_pairs - 1
         st_floor(q, nc.vector)

@@ -19,6 +19,7 @@ B_ROWS = 1024
 D_ROWS = 4096
 HALF = 512
 FLOPS = 2 * (B_ROWS + D_ROWS) * K * F
+LATE = 17
 
 
 def tile_minerva_detex_pa_kernel(tc, features, ex_features_bytes, ex_features_scale, gW, gb, out_0, out_1):
@@ -187,6 +188,10 @@ def tile_minerva_detex_pa_kernel(tc, features, ex_features_bytes, ex_features_sc
                         )
 
         def st_bias(q, a):
+            st_add(q, a)
+            st_square(q, a)
+
+        def st_add(q, a):
             if q not in zs:
                 zs[q] = zp.tile([P, 2, F], F32, name="z")
                 sums[q] = sp.tile([P, 2], F32, name="ss")
@@ -198,8 +203,31 @@ def tile_minerva_detex_pa_kernel(tc, features, ex_features_bytes, ex_features_sc
                     in1=bias_sb[:, nh * HALF:(nh + 1) * HALF],
                     op=ALU.add,
                 )
+
+        def st_square(q, a):
             junk = jp.tile([P, F], BF16, name="junk")
-            nc.scalar.activation(out=junk[:], in_=z[:, a, :], func=ACT.Square, accum_out=sums[q][:, a:a + 1])
+            nc.scalar.activation(out=junk[:], in_=zs[q][:, a, :], func=ACT.Square, accum_out=sums[q][:, a:a + 1])
+
+        def late_norm(q, a, eng):
+            sm = sp.tile([P, 1], F32, name="sm1")
+            eng.tensor_scalar(out=sm[:], in0=sums[q][:, a:a + 1], scalar1=1e-24, scalar2=None, op0=ALU.max)
+            ri = sp.tile([P, 1], F32, name="ri1")
+            nc.scalar.activation(out=ri[:], in_=sm[:], func=ACT.Abs_reciprocal_sqrt)
+            return ri
+
+        def late_scale(q, a, ri, who):
+            z = zs[q]
+            if who == "G":
+                nc.gpsimd.tensor_scalar(out=z[:, a, :], in0=z[:, a, :], scalar1=ri[:], scalar2=0.0, op0=ALU.mult, op1=ALU.add)
+                nc.sync.dma_start(out=out_rows(q, a), in_=z[:, a, :])
+            elif who == "V":
+                nc.vector.tensor_scalar(out=z[:, a, :], in0=z[:, a, :], scalar1=ri[:], scalar2=None, op0=ALU.mult)
+                nc.sync.dma_start(out=out_rows(q, a), in_=z[:, a, :])
+            else:
+                nc.scalar.activation(out=z[:, a, HALF:F], in_=z[:, a, HALF:F], func=ACT.Copy, scale=ri[:])
+                nc.sync.dma_start(out=out_rows(q, a)[:, HALF:F], in_=z[:, a, HALF:F])
+                nc.vector.tensor_scalar(out=z[:, a, 0:HALF], in0=z[:, a, 0:HALF], scalar1=ri[:], scalar2=None, op0=ALU.mult)
+                nc.sync.dma_start(out=out_rows(q, a)[:, 0:HALF], in_=z[:, a, 0:HALF])
 
         def st_floor(q, eng):
             sm = sp.tile([P, 2], F32, name="sm")
@@ -256,29 +284,25 @@ def tile_minerva_detex_pa_kernel(tc, features, ex_features_bytes, ex_features_sc
         st_cast(2, 2)
         st_mm(0)
 
-        for s in range(n_pairs):
-            last = s == n_pairs - 1
+        for s in range(LATE):
             plain_next = s + 2 < n_pairs and order[s + 2][0] == "f"
-            if s + 2 < n_pairs:
-                st_turn(s + 2, 0)
-                st_turn(s + 2, 1)
+            st_turn(s + 2, 0)
+            st_turn(s + 2, 1)
             if plain_next:
                 st_empty(s + 2, 0)
                 st_rnorm(s - 1)
                 st_scale(s - 1)
                 st_empty(s + 2, 1)
             st_bias(s, 0)
-            if s + 1 < n_pairs:
-                if s > 0:
-                    st_quant(s + 1)
-                st_mm(s + 1)
+            if s > 0:
+                st_quant(s + 1)
+            st_mm(s + 1)
             if s > 0 and not plain_next:
                 st_rnorm(s - 1)
                 st_scale(s - 1)
             st_bias(s, 1)
-            if not last:
-                st_floor(s, nc.gpsimd)
-            if s + 2 < n_pairs and not plain_next:
+            st_floor(s, nc.gpsimd)
+            if not plain_next:
                 st_empty(s + 2, 0)
                 st_empty(s + 2, 1)
             if s == 0:
@@ -288,14 +312,29 @@ def tile_minerva_detex_pa_kernel(tc, features, ex_features_bytes, ex_features_sc
             if s + 6 < n_pairs and order[s + 4][0] == "f":
                 st_cast(s + 6, 2)
 
+        tiles = [(q, a) for q in range(LATE, n_pairs) for a in range(2)]
+        st_turn(LATE + 2, 0)
+        st_turn(LATE + 2, 1)
+        st_empty(LATE + 2, 0)
+        st_rnorm(LATE - 1)
+        st_scale(LATE - 1)
+        st_empty(LATE + 2, 1)
+        for i in range(len(tiles) - 1):
+            q, a = tiles[i]
+            st_bias(q, a)
+            if a == 0 and q + 1 < n_pairs:
+                st_quant(q + 1)
+                st_mm(q + 1)
+            if i >= 1:
+                q, a = tiles[i - 1]
+                ri = late_norm(q, a, nc.vector)
+                if i < len(tiles) - 2:
+                    late_scale(q, a, ri, "G")
         q = n_pairs - 1
-        st_floor(q, nc.vector)
-        st_rnorm(q)
-        z = zs[q]
-        ri = rinvs[q]
-        nc.vector.tensor_scalar(out=z[:, 0, :], in0=z[:, 0, :], scalar1=ri[:, 0:1], scalar2=None, op0=ALU.mult)
-        nc.sync.dma_start(out=out_rows(q, 0), in_=z[:, 0, :])
-        nc.scalar.activation(out=z[:, 1, HALF:F], in_=z[:, 1, HALF:F], func=ACT.Copy, scale=ri[:, 1:2])
-        nc.sync.dma_start(out=out_rows(q, 1)[:, HALF:F], in_=z[:, 1, HALF:F])
-        nc.vector.tensor_scalar(out=z[:, 1, 0:HALF], in0=z[:, 1, 0:HALF], scalar1=ri[:, 1:2], scalar2=None, op0=ALU.mult)
-        nc.sync.dma_start(out=out_rows(q, 1)[:, 0:HALF], in_=z[:, 1, 0:HALF])
+        st_add(q, 1)
+        ri0 = late_norm(q, 0, nc.vector)
+        late_scale(q - 1, 1, ri, "V")
+        st_square(q, 1)
+        late_scale(q, 0, ri0, "V")
+        ri = late_norm(q, 1, nc.vector)
+        late_scale(q, 1, ri, "VS")

@@ -27,7 +27,7 @@ def tile_minerva_detex_pa_kernel(tc, features, ex_features_bytes, ex_features_sc
     with ExitStack() as ctx:
         keep = ctx.enter_context(tc.tile_pool(name="keep", bufs=1))
         wide = ctx.enter_context(tc.tile_pool(name="wide", bufs=8))
-        grp = ctx.enter_context(tc.tile_pool(name="grp", bufs=3))
+        grp = ctx.enter_context(tc.tile_pool(name="grp", bufs=4))
         cod = ctx.enter_context(tc.tile_pool(name="cod", bufs=3))
         zp = ctx.enter_context(tc.tile_pool(name="zp", bufs=6))
         jp = ctx.enter_context(tc.tile_pool(name="jp", bufs=2))
@@ -285,37 +285,41 @@ def tile_minerva_detex_pa_kernel(tc, features, ex_features_bytes, ex_features_sc
         st_mm(0)
 
         for s in range(LATE):
-            plain_next = s + 2 < n_pairs and order[s + 2][0] == "f"
-            st_turn(s + 2, 0)
-            st_turn(s + 2, 1)
-            if plain_next:
-                st_empty(s + 2, 0)
+            if s < 2:
+                now = [(s + 2, 0), (s + 2, 1)]
+            elif s == 2:
+                now = [(4, 0), (5, 0), (4, 1)]
+            else:
+                now = [(s + 2, 1), (s + 3, 0)]
+            plain = [t for t in now if order[t[0]][0] == "f"]
+            scaled = [t for t in now if order[t[0]][0] == "e"]
+            for q, a in now[0:2]:
+                st_turn(q, a)
+            if plain:
+                st_empty(plain[0][0], plain[0][1])
                 st_rnorm(s - 1)
                 st_scale(s - 1)
-                st_empty(s + 2, 1)
             st_bias(s, 0)
             if s > 0:
                 st_quant(s + 1)
             st_mm(s + 1)
-            if s > 0 and not plain_next:
+            for q, a in now[2:]:
+                st_turn(q, a)
+                st_empty(q, a)
+            if s > 0 and not plain:
                 st_rnorm(s - 1)
                 st_scale(s - 1)
             st_bias(s, 1)
             st_floor(s, nc.gpsimd)
-            if not plain_next:
-                st_empty(s + 2, 0)
-                st_empty(s + 2, 1)
+            for q, a in scaled:
+                st_empty(q, a)
             if s == 0:
                 st_cast(3, 2)
-            if s + 4 < n_pairs and order[s + 4][0] == "e" and not plain_next:
-                st_cast(s + 4, 2)
-            if s + 6 < n_pairs and order[s + 4][0] == "f":
-                st_cast(s + 6, 2)
+            if s + 5 < n_pairs and order[s + 5][0] == "e":
+                st_cast(s + 5, 2)
 
         tiles = [(q, a) for q in range(LATE, n_pairs) for a in range(2)]
-        st_turn(LATE + 2, 0)
         st_turn(LATE + 2, 1)
-        st_empty(LATE + 2, 0)
         st_rnorm(LATE - 1)
         st_scale(LATE - 1)
         st_empty(LATE + 2, 1)

@@ -19,7 +19,7 @@ B_ROWS = 1024
 D_ROWS = 4096
 HALF = 512
 FLOPS = 2 * (B_ROWS + D_ROWS) * K * F
-LATE = 17
+LATE = 18
 
 
 def tile_minerva_detex_pa_kernel(tc, features, ex_features_bytes, ex_features_scale, gW, gb, out_0, out_1):
@@ -38,10 +38,9 @@ def tile_minerva_detex_pa_kernel(tc, features, ex_features_bytes, ex_features_sc
 
         order = []
         for i in range(4):
-            for c in (2 * i, 2 * i + 1):
-                order.append(("e", c, 0))
-                order.append(("e", c, 1))
-            order.append(("f", i // 2, i % 2))
+            four = [("e", c, h) for c in (2 * i, 2 * i + 1) for h in range(2)]
+            behind = 4 if i < 3 else 2
+            order.extend(four[0:behind] + [("f", i // 2, i % 2)] + four[behind:4])
         n_pairs = len(order)
 
         sc4 = keep.tile([P, 2, 4], F32, name="sc4")
@@ -75,6 +74,11 @@ def tile_minerva_detex_pa_kernel(tc, features, ex_features_bytes, ex_features_sc
         make_identity(nc, ident[:])
         one = keep.tile([P, 1], F32, name="one")
         nc.vector.memset(one[:], 1.0)
+        eps_neg = keep.tile([P, 1], F32, name="eps_neg")
+        nc.vector.memset(eps_neg[:], -1e-24)
+        eps_pos = keep.tile([P, 1], F32, name="eps_pos")
+        nc.vector.memset(eps_pos[:], 1e-24)
+        gate = keep.tile([P, 1], U32, name="gate")
         warm = keep.tile([P, 1], F32, name="warm")
         nc.scalar.activation(out=warm[:], in_=one[:], func=ACT.Abs_reciprocal_sqrt)
 
@@ -130,7 +134,6 @@ def tile_minerva_detex_pa_kernel(tc, features, ex_features_bytes, ex_features_sc
         accs = {}
         zs = {}
         sums = {}
-        floors = {}
         rinvs = {}
 
         def st_cast(q, tiles):
@@ -208,12 +211,15 @@ def tile_minerva_detex_pa_kernel(tc, features, ex_features_bytes, ex_features_sc
             junk = jp.tile([P, F], BF16, name="junk")
             nc.scalar.activation(out=junk[:], in_=zs[q][:, a, :], func=ACT.Square, accum_out=sums[q][:, a:a + 1])
 
-        def late_norm(q, a, eng):
-            sm = sp.tile([P, 1], F32, name="sm1")
-            eng.tensor_scalar(out=sm[:], in0=sums[q][:, a:a + 1], scalar1=1e-24, scalar2=None, op0=ALU.max)
-            ri = sp.tile([P, 1], F32, name="ri1")
-            nc.scalar.activation(out=ri[:], in_=sm[:], func=ACT.Abs_reciprocal_sqrt)
+        def norm_factor(ss, width, tag):
+            rl = sp.tile([P, width], F32, name="rl" + tag)
+            nc.scalar.activation(out=rl[:], in_=ss, func=ACT.Relu, bias=eps_neg[:])
+            ri = sp.tile([P, width], F32, name="ri" + tag)
+            nc.scalar.activation(out=ri[:], in_=rl[:], func=ACT.Abs_reciprocal_sqrt, bias=eps_pos[:])
             return ri
+
+        def late_norm(q, a):
+            return norm_factor(sums[q][:, a:a + 1], 1, "1")
 
         def late_scale(q, a, ri, who):
             z = zs[q]
@@ -229,15 +235,11 @@ def tile_minerva_detex_pa_kernel(tc, features, ex_features_bytes, ex_features_sc
                 nc.vector.tensor_scalar(out=z[:, a, 0:HALF], in0=z[:, a, 0:HALF], scalar1=ri[:], scalar2=None, op0=ALU.mult)
                 nc.sync.dma_start(out=out_rows(q, a)[:, 0:HALF], in_=z[:, a, 0:HALF])
 
-        def st_floor(q, eng):
-            sm = sp.tile([P, 2], F32, name="sm")
-            eng.tensor_scalar(out=sm[:], in0=sums[q][:], scalar1=1e-24, scalar2=None, op0=ALU.max)
-            floors[q] = sm
-
         def st_rnorm(q):
-            ri = sp.tile([P, 2], F32, name="ri")
-            nc.scalar.activation(out=ri[:], in_=floors[q][:], func=ACT.Abs_reciprocal_sqrt)
-            rinvs[q] = ri
+            rinvs[q] = norm_factor(sums[q][:], 2, "2")
+
+        def st_gate(q):
+            nc.gpsimd.tensor_copy(out=gate[:], in_=codes[q][0][:, 0:1])
 
         def out_rows(q, a):
             kind, c, h = order[q]
@@ -290,55 +292,45 @@ def tile_minerva_detex_pa_kernel(tc, features, ex_features_bytes, ex_features_sc
             elif s == 2:
                 now = [(4, 0), (5, 0), (4, 1)]
             else:
-                now = [(s + 2, 1), (s + 3, 0)]
-            plain = [t for t in now if order[t[0]][0] == "f"]
-            scaled = [t for t in now if order[t[0]][0] == "e"]
+                now = [(q, a) for q, a in ((s + 2, 1), (s + 3, 0)) if q < n_pairs]
             for q, a in now[0:2]:
                 st_turn(q, a)
-            if plain:
-                st_empty(plain[0][0], plain[0][1])
-                st_rnorm(s - 1)
-                st_scale(s - 1)
+                if order[q][0] == "f":
+                    st_empty(q, a)
             st_bias(s, 0)
             if s > 0:
                 st_quant(s + 1)
+                st_gate(s + 1)
+                st_scale(s - 1)
             st_mm(s + 1)
             for q, a in now[2:]:
                 st_turn(q, a)
                 st_empty(q, a)
-            if s > 0 and not plain:
-                st_rnorm(s - 1)
-                st_scale(s - 1)
             st_bias(s, 1)
-            st_floor(s, nc.gpsimd)
-            for q, a in scaled:
-                st_empty(q, a)
+            st_rnorm(s)
+            for q, a in now[0:2]:
+                if order[q][0] == "e":
+                    st_empty(q, a)
             if s == 0:
                 st_cast(3, 2)
             if s + 5 < n_pairs and order[s + 5][0] == "e":
                 st_cast(s + 5, 2)
 
-        tiles = [(q, a) for q in range(LATE, n_pairs) for a in range(2)]
-        st_turn(LATE + 2, 1)
-        st_rnorm(LATE - 1)
-        st_scale(LATE - 1)
-        st_empty(LATE + 2, 1)
-        for i in range(len(tiles) - 1):
-            q, a = tiles[i]
-            st_bias(q, a)
-            if a == 0 and q + 1 < n_pairs:
-                st_quant(q + 1)
-                st_mm(q + 1)
-            if i >= 1:
-                q, a = tiles[i - 1]
-                ri = late_norm(q, a, nc.vector)
-                if i < len(tiles) - 2:
-                    late_scale(q, a, ri, "G")
         q = n_pairs - 1
+        st_bias(q - 1, 0)
+        st_quant(q)
+        st_gate(q)
+        st_scale(q - 2)
+        st_mm(q)
+        ri = late_norm(q - 1, 0)
+        late_scale(q - 1, 0, ri, "G")
+        st_bias(q - 1, 1)
+        ri1 = late_norm(q - 1, 1)
+        st_bias(q, 0)
         st_add(q, 1)
-        ri0 = late_norm(q, 0, nc.vector)
-        late_scale(q - 1, 1, ri, "V")
+        late_scale(q - 1, 1, ri1, "V")
+        ri0 = late_norm(q, 0)
         st_square(q, 1)
         late_scale(q, 0, ri0, "V")
-        ri = late_norm(q, 1, nc.vector)
+        ri = late_norm(q, 1)
         late_scale(q, 1, ri, "VS")

@@ -74,10 +74,6 @@ def tile_minerva_detex_pa_kernel(tc, features, ex_features_bytes, ex_features_sc
         make_identity(nc, ident[:])
         one = keep.tile([P, 1], F32, name="one")
         nc.vector.memset(one[:], 1.0)
-        eps_neg = keep.tile([P, 1], F32, name="eps_neg")
-        nc.vector.memset(eps_neg[:], -1e-24)
-        eps_pos = keep.tile([P, 1], F32, name="eps_pos")
-        nc.vector.memset(eps_pos[:], 1e-24)
         gate = keep.tile([P, 1], U32, name="gate")
         warm = keep.tile([P, 1], F32, name="warm")
         nc.scalar.activation(out=warm[:], in_=one[:], func=ACT.Abs_reciprocal_sqrt)
@@ -213,9 +209,9 @@ def tile_minerva_detex_pa_kernel(tc, features, ex_features_bytes, ex_features_sc
 
         def norm_factor(ss, width, tag):
             rl = sp.tile([P, width], F32, name="rl" + tag)
-            nc.scalar.activation(out=rl[:], in_=ss, func=ACT.Relu, bias=eps_neg[:])
+            nc.scalar.activation(out=rl[:], in_=ss, func=ACT.Relu, bias=-1e-24)
             ri = sp.tile([P, width], F32, name="ri" + tag)
-            nc.scalar.activation(out=ri[:], in_=rl[:], func=ACT.Abs_reciprocal_sqrt, bias=eps_pos[:])
+            nc.scalar.activation(out=ri[:], in_=rl[:], func=ACT.Abs_reciprocal_sqrt, bias=1e-24)
             return ri
 
         def late_norm(q, a):

from contextlib import ExitStack

import concourse.mybir as mybir
from concourse.masks import make_identity

F32 = mybir.dt.float32
BF16 = mybir.dt.bfloat16
U32 = mybir.dt.uint32
U8 = mybir.dt.uint8
FP8 = mybir.dt.float8_e4m3fn
FP8X4 = mybir.dt.float8_e4m3fn_x4
ALU = mybir.AluOpType
ACT = mybir.ActivationFunctionType

P = 128
K = 1024
F = 1024
B_ROWS = 1024
D_ROWS = 4096
HALF = 512
FLOPS = 2 * (B_ROWS + D_ROWS) * K * F
LATE = 18


def tile_minerva_detex_pa_kernel(tc, features, ex_features_bytes, ex_features_scale, gW, gb, out_0, out_1):
    nc = tc.nc
    with ExitStack() as ctx:
        keep = ctx.enter_context(tc.tile_pool(name="keep", bufs=1))
        wide = ctx.enter_context(tc.tile_pool(name="wide", bufs=8))
        grp = ctx.enter_context(tc.tile_pool(name="grp", bufs=4))
        cod = ctx.enter_context(tc.tile_pool(name="cod", bufs=3))
        zp = ctx.enter_context(tc.tile_pool(name="zp", bufs=6))
        jp = ctx.enter_context(tc.tile_pool(name="jp", bufs=2))
        sp = ctx.enter_context(tc.tile_pool(name="sp", bufs=4))
        ps_t = ctx.enter_context(tc.psum_pool(name="ps_t", bufs=2))
        ps_a = ctx.enter_context(tc.psum_pool(name="ps_a", bufs=6))
        ctx.enter_context(tc.manual_schedule())

        order = []
        for i in range(4):
            four = [("e", c, h) for c in (2 * i, 2 * i + 1) for h in range(2)]
            behind = 4 if i < 3 else 2
            order.extend(four[0:behind] + [("f", i // 2, i % 2)] + four[behind:4])
        n_pairs = len(order)

        sc4 = keep.tile([P, 2, 4], F32, name="sc4")
        ex_view = ex_features_bytes.rearrange("(c p n) k -> c p (n k)", p=P, n=4)
        ex_first = [
            keep.tile([P, K], U8, name="ex_first0"),
            keep.tile([P, K], U8, name="ex_first1"),
            keep.tile([P, 2 * K], U8, name="ex_first2"),
        ]
        ex_raw = [None] + [keep.tile([P, 4 * K], U8, name="ex_raw%d" % c) for c in range(1, 8)]
        f_view = features.rearrange("(c p n) k -> c p n k", p=P, n=4)
        f_raw = [keep.tile([P, 2, K], BF16, name="f_raw%d" % q) for q in range(4)]
        w_view = gW.rearrange("(j p) k -> p j k", p=P)
        w_raw = [keep.tile([P, 2, K], BF16, name="w_raw%d" % i) for i in range(4)]
        bias_sb = keep.tile([P, F], BF16, name="bias_sb")
        nc.sync.dma_start(out=ex_first[0][:], in_=ex_view[0][:, 0:K])
        nc.sync.dma_start(out=sc4[:], in_=ex_features_scale.rearrange("o (g p t) -> p (o g) t", g=2, p=P, t=4))
        nc.sync.dma_start(out=ex_first[1][:], in_=ex_view[0][:, K:2 * K])
        nc.sync.dma_start(out=ex_first[2][:], in_=ex_view[0][:, 2 * K:4 * K])
        for i in range(4):
            nc.sync.dma_start(out=w_raw[i][:], in_=w_view[:, 2 * i:2 * i + 2, :])
        nc.sync.dma_start(out=bias_sb[:], in_=gb.partition_broadcast(P))
        nc.sync.dma_start(out=ex_raw[1][:], in_=ex_view[1])
        for i in range(4):
            nc.sync.dma_start(out=f_raw[i][:], in_=f_view[i // 2][:, 2 * (i % 2):2 * (i % 2) + 2, :])
            if i < 3:
                nc.sync.dma_start(out=ex_raw[2 * i + 2][:], in_=ex_view[2 * i + 2])
                nc.sync.dma_start(out=ex_raw[2 * i + 3][:], in_=ex_view[2 * i + 3])

        ident = keep.tile([P, P], F32, name="ident")
        make_identity(nc, ident[:])
        one = keep.tile([P, 1], F32, name="one")
        nc.vector.memset(one[:], 1.0)
        gate = keep.tile([P, 1], U32, name="gate")
        warm = keep.tile([P, 1], F32, name="warm")
        nc.scalar.activation(out=warm[:], in_=one[:], func=ACT.Abs_reciprocal_sqrt)

        sc_bc = sc4[:].rearrange("p g (u e) -> p g u e", u=2).unsqueeze(2).to_broadcast([P, 2, P, 2, 2])

        def turn(bank, words):
            for g in range(2):
                for u in range(2):
                    nc.tensor.transpose(
                        bank[:, (2 * u + g) * P:(2 * u + g + 1) * P],
                        words[:, 256 * g + u:256 * (g + 1):2],
                        ident[:],
                    )

        def empty(bank, dst):
            nc.scalar.copy(out=dst.bitcast(F32), in_=bank[:].rearrange("p (u g r) -> p g r u", u=2, g=2))

        def empty_scaled(bank, dst):
            nc.vector.tensor_tensor(
                out=dst.rearrange("p g r (u e) -> p g r u e", u=2),
                in0=bank[:].bitcast(BF16).rearrange("p (u g r e) -> p g r u e", u=2, g=2, e=2),
                in1=sc_bc,
                op=ALU.mult,
            )

        w_grp = [keep.tile([P, 2, HALF, 4], BF16, name="w_grp%d" % nh, align_bytes=64) for nh in range(2)]
        w_cod = [keep.tile([P, 2, HALF], U32, name="w_cod%d" % nh, align_bytes=64) for nh in range(2)]
        w_scl = [keep.tile([P, 2, HALF], U8, name="w_scl%d" % nh, align_bytes=64) for nh in range(2)]
        w_bank = {}

        def w_turn(j):
            bank = ps_a.tile([P, HALF], F32, name="acc")
            w_bank[j] = bank
            turn(bank, w_raw[j // 2][:, j % 2, :].bitcast(F32))

        def w_empty(j):
            empty(w_bank[j], w_grp[j // 4][:, :, (j % 4) * P:(j % 4 + 1) * P, :])

        def w_quant(nh):
            for g in range(2):
                nc.vector.quantize_mx(
                    out=w_cod[nh][:, g, :].bitcast(FP8X4),
                    scales=w_scl[nh][:, g, :],
                    in_=w_grp[nh][:, g].rearrange("p n t -> p (n t)"),
                )

        o0_view = out_0.rearrange("(c p n) f -> c p n f", p=P, n=4)
        o1_view = out_1.rearrange("(c p n) f -> c p n f", p=P, n=4)
        xb = {}
        banks = {}
        grouped = {}
        codes = {}
        accs = {}
        zs = {}
        sums = {}
        rinvs = {}

        def st_cast(q, tiles):
            kind, c, h = order[q]
            if q not in xb:
                xb[q] = wide.tile([P, 2, K], BF16, name="xb")
            t = xb[q]
            if tiles == 2:
                nc.scalar.copy(out=t[:].rearrange("p a k -> p (a k)"), in_=ex_raw[c][:, 2 * h * K:(2 * h + 2) * K].bitcast(FP8))
            elif q == 0:
                nc.vector.tensor_copy(out=t[:, tiles, :], in_=ex_first[tiles][:].bitcast(FP8))
            else:
                nc.scalar.copy(out=t[:, tiles, :], in_=ex_first[2][:, tiles * K:(tiles + 1) * K].bitcast(FP8))

        def st_turn(q, a):
            kind, c, h = order[q]
            if kind == "f":
                words = f_raw[2 * c + h][:, a, :].bitcast(F32)
            else:
                words = xb[q][:, a, :].bitcast(F32)
            bank = ps_t.tile([P, HALF], F32, name="bank")
            banks[(q, a)] = bank
            turn(bank, words)

        def st_empty(q, a):
            if q not in grouped:
                grouped[q] = grp.tile([P, 2, 2, P, 4], BF16, name="gt", align_bytes=64)
            if order[q][0] == "f":
                empty(banks[(q, a)], grouped[q][:, a])
            else:
                empty_scaled(banks[(q, a)], grouped[q][:, a])

        def st_quant(q):
            xc = cod.tile([P, 4 * P], U32, name="xc", align_bytes=64)
            xs = cod.tile([P, 4 * P], U8, name="xs", align_bytes=64)
            nc.vector.quantize_mx(out=xc[:].bitcast(FP8X4), scales=xs[:], in_=grouped[q][:].rearrange("p a g r t -> p (a g r t)"))
            codes[q] = (xc, xs)

        def st_mm(q):
            xc, xs = codes[q]
            for a in range(2):
                for nh in range(2):
                    acc = ps_a.tile([P, HALF], F32, name="acc")
                    accs[(q, a, nh)] = acc
                    for g in range(2):
                        cols = slice((2 * a + g) * P, (2 * a + g + 1) * P)
                        nc.tensor.matmul_mx(
                            out=acc[:],
                            lhsT=xc[:, cols].bitcast(FP8X4),
                            lhsT_scale=xs[:, cols],
                            rhs=w_cod[nh][:, g, :].bitcast(FP8X4),
                            rhs_scale=w_scl[nh][:, g, :],
                            start=(g == 0),
                            stop=(g == 1),
                        )

        def st_bias(q, a):
            st_add(q, a)
            st_square(q, a)

        def st_add(q, a):
            if q not in zs:
                zs[q] = zp.tile([P, 2, F], F32, name="z")
                sums[q] = sp.tile([P, 2], F32, name="ss")
            z = zs[q]
            for nh in range(2):
                nc.vector.tensor_tensor(
                    out=z[:, a, nh * HALF:(nh + 1) * HALF],
                    in0=accs[(q, a, nh)][:],
                    in1=bias_sb[:, nh * HALF:(nh + 1) * HALF],
                    op=ALU.add,
                )

        def st_square(q, a):
            junk = jp.tile([P, F], BF16, name="junk")
            nc.scalar.activation(out=junk[:], in_=zs[q][:, a, :], func=ACT.Square, accum_out=sums[q][:, a:a + 1])

        def norm_factor(ss, width, tag):
            rl = sp.tile([P, width], F32, name="rl" + tag)
            nc.scalar.activation(out=rl[:], in_=ss, func=ACT.Relu, bias=-1e-24)
            ri = sp.tile([P, width], F32, name="ri" + tag)
            nc.scalar.activation(out=ri[:], in_=rl[:], func=ACT.Abs_reciprocal_sqrt, bias=1e-24)
            return ri

        def late_norm(q, a):
            return norm_factor(sums[q][:, a:a + 1], 1, "1")

        def late_scale(q, a, ri, who):
            z = zs[q]
            if who == "G":
                nc.gpsimd.tensor_scalar(out=z[:, a, :], in0=z[:, a, :], scalar1=ri[:], scalar2=0.0, op0=ALU.mult, op1=ALU.add)
                nc.sync.dma_start(out=out_rows(q, a), in_=z[:, a, :])
            elif who == "V":
                nc.vector.tensor_scalar(out=z[:, a, :], in0=z[:, a, :], scalar1=ri[:], scalar2=None, op0=ALU.mult)
                nc.sync.dma_start(out=out_rows(q, a), in_=z[:, a, :])
            else:
                nc.scalar.activation(out=z[:, a, HALF:F], in_=z[:, a, HALF:F], func=ACT.Copy, scale=ri[:])
                nc.sync.dma_start(out=out_rows(q, a)[:, HALF:F], in_=z[:, a, HALF:F])
                nc.vector.tensor_scalar(out=z[:, a, 0:HALF], in0=z[:, a, 0:HALF], scalar1=ri[:], scalar2=None, op0=ALU.mult)
                nc.sync.dma_start(out=out_rows(q, a)[:, 0:HALF], in_=z[:, a, 0:HALF])

        def st_rnorm(q):
            rinvs[q] = norm_factor(sums[q][:], 2, "2")

        def st_gate(q):
            nc.gpsimd.tensor_copy(out=gate[:], in_=codes[q][0][:, 0:1])

        def out_rows(q, a):
            kind, c, h = order[q]
            view = o0_view if kind == "f" else o1_view
            return view[c][:, 2 * h + a, :]

        def st_scale(q):
            z = zs[q]
            ri = rinvs[q]
            for a in range(2):
                nc.gpsimd.tensor_scalar(out=z[:, a, :], in0=z[:, a, :], scalar1=ri[:, a:a + 1], scalar2=0.0, op0=ALU.mult, op1=ALU.add)
                nc.sync.dma_start(out=out_rows(q, a), in_=z[:, a, :])

        st_cast(0, 0)
        st_cast(0, 1)
        st_turn(0, 0)
        st_empty(0, 0)
        st_turn(0, 1)
        st_empty(0, 1)
        st_cast(1, 0)
        st_cast(1, 1)
        w_turn(0)
        w_turn(1)
        st_quant(0)
        st_turn(1, 0)
        st_empty(1, 0)
        w_turn(2)
        w_turn(3)
        st_turn(1, 1)
        st_empty(1, 1)
        w_turn(4)
        w_turn(5)
        w_empty(0)
        w_turn(6)
        w_empty(1)
        w_turn(7)
        w_empty(2)
        w_empty(3)
        st_quant(1)
        w_quant(0)
        for j in range(4, 8):
            w_empty(j)
        w_quant(1)
        st_cast(2, 2)
        st_mm(0)

        for s in range(LATE):
            if s < 2:
                now = [(s + 2, 0), (s + 2, 1)]
            elif s == 2:
                now = [(4, 0), (5, 0), (4, 1)]
            else:
                now = [(q, a) for q, a in ((s + 2, 1), (s + 3, 0)) if q < n_pairs]
            for q, a in now[0:2]:
                st_turn(q, a)
                if order[q][0] == "f":
                    st_empty(q, a)
            st_bias(s, 0)
            if s > 0:
                st_quant(s + 1)
                st_gate(s + 1)
                st_scale(s - 1)
            st_mm(s + 1)
            for q, a in now[2:]:
                st_turn(q, a)
                st_empty(q, a)
            st_bias(s, 1)
            st_rnorm(s)
            for q, a in now[0:2]:
                if order[q][0] == "e":
                    st_empty(q, a)
            if s == 0:
                st_cast(3, 2)
            if s + 5 < n_pairs and order[s + 5][0] == "e":
                st_cast(s + 5, 2)

        q = n_pairs - 1
        st_bias(q - 1, 0)
        st_quant(q)
        st_gate(q)
        st_scale(q - 2)
        st_mm(q)
        ri = late_norm(q - 1, 0)
        late_scale(q - 1, 0, ri, "G")
        st_bias(q - 1, 1)
        ri1 = late_norm(q - 1, 1)
        st_bias(q, 0)
        st_add(q, 1)
        late_scale(q - 1, 1, ri1, "V")
        ri0 = late_norm(q, 0)
        st_square(q, 1)
        late_scale(q, 0, ri0, "V")
        ri = late_norm(q, 1)
        late_scale(q, 1, ri, "VS")
